import numpy as np
import ml_dtypes

BF16 = ml_dtypes.bfloat16


def bf(x):
    return np.asarray(x, np.float32).astype(BF16)


def f32(x):
    return np.asarray(x, np.float32)


def f64(x):
    return np.asarray(x).astype(np.float64)


def striped(idx):
    return np.tile(idx.reshape(-1, 16).T, (8, 1))


F, S, OUT, NO, K, NDIST, NPHI, N = 128, 4096, 128, 64, 8, 2, 2, 512
A = NDIST * NPHI
DIST_MAX, SIGMA, KAPPA = 1.0, 0.5, 1.0
DISTS = np.linspace(0.0, DIST_MAX, NDIST)
PHIS = np.linspace(-np.pi, np.pi, NPHI + 1)[:-1]


def setup_inputs():
    return {"table": bf(np.random.standard_normal((F, S))), "w": bf(np.random.standard_normal((F, A * OUT)) / np.sqrt(F * A)), "d_dists": f32(np.random.uniform(0.0, DIST_MAX, (1, N))), "d_phi": f32(np.random.uniform(-np.pi, np.pi, (1, N))), "offs": striped(np.random.permutation(np.tile(np.arange(S), 2))[:N])}


def reference(table, w, d_dists, d_phi, offs):
    idx = offs[:16].T.reshape(-1)
    dd = f64(d_dists)[0]
    dp = f64(d_phi)[0]
    wd = np.exp(-0.5 * ((dd[None, :] - DISTS[:, None]) / SIGMA) ** 2)
    wp = np.exp(KAPPA * np.cos(dp[None, :] - PHIS[:, None]))
    u = (wd[:, None, :] * wp[None, :, :]).reshape(A, NO, K)
    kw = u / u.sum(axis=2, keepdims=True)
    proj = (f64(w).T @ f64(table)[:, idx]).reshape(A, OUT, NO, K)
    return np.einsum("aonk,ank->on", proj, kw)

@@ -1,0 +1,83 @@
+import concourse.mybir as mybir
+
+F32 = mybir.dt.float32
+BF16 = mybir.dt.bfloat16
+U16 = mybir.dt.uint16
+FUNC = mybir.ActivationFunctionType
+ALU = mybir.AluOpType
+AXIS = mybir.AxisListType
+
+P = 128
+S = 4096
+N = 512
+NODES = 64
+K = 8
+A = 4
+DIST = (0.0, 1.0)
+SIGN = (-1.0, 1.0)
+
+FLOPS = 2 * P * (A * P) * N
+
+
+def tile_nolayer_kernel(tc, table, w, d_dists, d_phi, offs, out):
+    nc = tc.nc
+    with (
+        tc.tile_pool(name="held", bufs=1) as held,
+        tc.psum_pool(name="banks", bufs=1) as banks,
+    ):
+        offsets = held.tile([P, N // 16], U16, name="offsets")
+        nc.sync.dma_start(offsets[:], offs)
+        phi = held.tile([P, N], F32, name="phi")
+        nc.scalar.dma_start(phi[:], d_phi.broadcast_to([P, N]))
+        dist = held.tile([P, N], F32, name="dist")
+        nc.gpsimd.dma_start(dist[:], d_dists.broadcast_to([P, N]))
+        weights = held.tile([P, A * P], BF16, name="weights")
+        nc.sync.dma_start(weights[:], w)
+        nodes = held.tile([P, S], BF16, name="nodes")
+        nc.sync.dma_start(nodes[:], table)
+
+        half_sin = held.tile([P, N], F32, name="half_sin")
+        nc.scalar.activation(half_sin[:], phi[:], FUNC.Sin, scale=0.5)
+        sin2 = held.tile([P, N], F32, name="sin2")
+        nc.vector.tensor_tensor(sin2[:], half_sin[:], half_sin[:], ALU.mult)
+        gap2 = held.tile([P, 2 * N], F32, name="gap2")
+        for i in range(2):
+            nc.scalar.activation(gap2[:, i * N : (i + 1) * N], dist[:], FUNC.Square, bias=-DIST[i])
+
+        u = held.tile([P, A * N], F32, name="u")
+        for a in range(A):
+            i, q = divmod(a, 2)
+            cols = slice(a * N, (a + 1) * N)
+            nc.vector.tensor_tensor(
+                u[:, cols], gap2[:, i * N : (i + 1) * N], sin2[:], ALU.add if SIGN[q] > 0 else ALU.subtract
+            )
+            nc.scalar.activation(u[:, cols], u[:, cols], FUNC.Exp, scale=-2.0, bias=SIGN[q])
+
+        groups = A * NODES
+        u_by_group = u[:].rearrange("p (g k) -> p g k", k=K)
+        total = held.tile([P, groups], F32, name="total")
+        nc.vector.tensor_reduce(total[:], u_by_group, AXIS.X, ALU.add)
+        inverse = held.tile([P, groups], F32, name="inverse")
+        nc.vector.reciprocal(inverse[:], total[:])
+        kw = held.tile([P, A * N], F32, name="kw")
+        nc.vector.tensor_tensor(
+            kw[:].rearrange("p (g k) -> p g k", k=K),
+            u_by_group,
+            inverse[:].unsqueeze(2).to_broadcast([P, groups, K]),
+            ALU.mult,
+        )
+
+        weighted = held.tile([P, A * N], F32, name="weighted")
+        for a in range(A):
+            cols = slice(a * N, (a + 1) * N)
+            proj = banks.tile([P, N], F32, name=f"proj{a}")
+            nc.tensor.matmul(
+                proj[:], weights[:, a * P : (a + 1) * P], nodes[:].indirect(offsets[:]), start=True, stop=True
+            )
+            nc.vector.tensor_tensor(weighted[:, cols], proj[:], kw[:, cols], ALU.mult)
+
+        result = held.tile([P, NODES], F32, name="result")
+        nc.vector.tensor_reduce(
+            result[:], weighted[:].rearrange("p (a n k) -> p n a k", a=A, k=K), AXIS.XY, ALU.add
+        )
+        nc.sync.dma_start(out, result[:])

@@ -1,4 +1,5 @@
 import concourse.mybir as mybir
+from concourse.masks import make_identity
 
 F32 = mybir.dt.float32
 BF16 = mybir.dt.bfloat16
@@ -15,8 +16,34 @@ K = 8
 A = 4
 DIST = (0.0, 1.0)
 SIGN = (-1.0, 1.0)
+SHIFT = tuple(SIGN[a % 2] - 2.0 * DIST[a // 2] ** 2 for a in range(A))
 
 FLOPS = 2 * P * (A * P) * N
+
+
+def weight_exponents(nc, pool, phi, dist, engines, label):
+    rows, cols = phi.shape
+    half_sin = pool.tile([rows, cols], F32, name=label + "_half_sin")
+    nc.scalar.activation(half_sin[:], phi[:], FUNC.Sin, scale=0.5)
+    sin2 = pool.tile([rows, cols], F32, name=label + "_sin2")
+    nc.vector.tensor_tensor(sin2[:], half_sin[:], half_sin[:], ALU.mult)
+    gaps = [pool.tile([rows, cols], F32, name=f"{label}_gap{i}") for i in range(2)]
+    for i in range(2):
+        nc.vector.scalar_tensor_tensor(gaps[i][:], dist[:], -2.0 * DIST[i], dist[:], ALU.add, ALU.mult)
+    x = pool.tile([rows, A * cols], F32, name=label + "_x")
+    for a in range(A):
+        i, q = divmod(a, 2)
+        add_or_subtract = ALU.add if SIGN[q] > 0 else ALU.subtract
+        engines[i].tensor_tensor(x[:, a * cols : (a + 1) * cols], gaps[i][:], sin2[:], add_or_subtract)
+    return x
+
+
+def exponentials(nc, x):
+    cols = x.shape[1] // A
+    for a in range(A):
+        x_a = x[:, a * cols : (a + 1) * cols]
+        nc.scalar.activation(x_a, x_a, FUNC.Exp, scale=-2.0, bias=SHIFT[a])
+    return x
 
 
 def tile_nolayer_kernel(tc, table, w, d_dists, d_phi, offs, out):
@@ -25,59 +52,61 @@ def tile_nolayer_kernel(tc, table, w, d_dists, d_phi, offs, out):
         tc.tile_pool(name="held", bufs=1) as held,
         tc.psum_pool(name="banks", bufs=1) as banks,
     ):
+        phi = held.tile([P, N], F32, name="phi")
+        nc.sync.dma_start(phi[:], d_phi.broadcast_to([P, N]))
+        dist = held.tile([P, N], F32, name="dist")
+        nc.scalar.dma_start(dist[:], d_dists.broadcast_to([P, N]))
+        phi_by_node = held.tile([NODES, K], F32, name="phi_by_node")
+        nc.sync.dma_start(phi_by_node[:], d_phi.rearrange("o (n k) -> (o n) k", k=K))
+        dist_by_node = held.tile([NODES, K], F32, name="dist_by_node")
+        nc.scalar.dma_start(dist_by_node[:], d_dists.rearrange("o (n k) -> (o n) k", k=K))
         offsets = held.tile([P, N // 16], U16, name="offsets")
         nc.sync.dma_start(offsets[:], offs)
-        phi = held.tile([P, N], F32, name="phi")
-        nc.scalar.dma_start(phi[:], d_phi.broadcast_to([P, N]))
-        dist = held.tile([P, N], F32, name="dist")
-        nc.gpsimd.dma_start(dist[:], d_dists.broadcast_to([P, N]))
         weights = held.tile([P, A * P], BF16, name="weights")
-        nc.sync.dma_start(weights[:], w)
+        nc.scalar.dma_start(weights[:], w)
         nodes = held.tile([P, S], BF16, name="nodes")
         nc.sync.dma_start(nodes[:], table)
 
-        half_sin = held.tile([P, N], F32, name="half_sin")
-        nc.scalar.activation(half_sin[:], phi[:], FUNC.Sin, scale=0.5)
-        sin2 = held.tile([P, N], F32, name="sin2")
-        nc.vector.tensor_tensor(sin2[:], half_sin[:], half_sin[:], ALU.mult)
-        gap2 = held.tile([P, 2 * N], F32, name="gap2")
-        for i in range(2):
-            nc.scalar.activation(gap2[:, i * N : (i + 1) * N], dist[:], FUNC.Square, bias=-DIST[i])
+        identity = held.tile([P, P], F32, name="identity")
+        make_identity(nc, identity[:])
+        ones = held.tile([P, P], F32, name="ones")
+        nc.gpsimd.memset(ones[:], 1.0)
+        spread = held.tile([P, A * NODES], F32, name="spread")
+        nc.gpsimd.memset(spread[:], 0.0)
 
-        u = held.tile([P, A * N], F32, name="u")
-        for a in range(A):
-            i, q = divmod(a, 2)
-            cols = slice(a * N, (a + 1) * N)
-            nc.vector.tensor_tensor(
-                u[:, cols], gap2[:, i * N : (i + 1) * N], sin2[:], ALU.add if SIGN[q] > 0 else ALU.subtract
-            )
-            nc.scalar.activation(u[:, cols], u[:, cols], FUNC.Exp, scale=-2.0, bias=SIGN[q])
+        x_by_node = weight_exponents(nc, held, phi_by_node, dist_by_node, (nc.vector, nc.vector), "node")
+        x = weight_exponents(nc, held, phi, dist, (nc.vector, nc.gpsimd), "all")
+        u_by_node = exponentials(nc, x_by_node)
+        u = exponentials(nc, x)
 
-        groups = A * NODES
-        u_by_group = u[:].rearrange("p (g k) -> p g k", k=K)
-        total = held.tile([P, groups], F32, name="total")
-        nc.vector.tensor_reduce(total[:], u_by_group, AXIS.X, ALU.add)
-        inverse = held.tile([P, groups], F32, name="inverse")
+        total = held.tile([NODES, A], F32, name="total")
+        nc.vector.tensor_reduce(total[:], u_by_node[:].rearrange("n (a k) -> n a k", k=K), AXIS.X, ALU.add)
+        inverse = held.tile([NODES, A], F32, name="inverse")
         nc.vector.reciprocal(inverse[:], total[:])
-        kw = held.tile([P, A * N], F32, name="kw")
         nc.vector.tensor_tensor(
-            kw[:].rearrange("p (g k) -> p g k", k=K),
-            u_by_group,
-            inverse[:].unsqueeze(2).to_broadcast([P, groups, K]),
+            spread[:NODES].rearrange("n (a c) -> n a c", a=A),
+            identity[:NODES, :NODES].unsqueeze(1).to_broadcast([NODES, A, NODES]),
+            inverse[:].unsqueeze(2).to_broadcast([NODES, A, NODES]),
             ALU.mult,
         )
 
         weighted = held.tile([P, A * N], F32, name="weighted")
+        summed = held.tile([P, A * NODES], F32, name="summed")
         for a in range(A):
-            cols = slice(a * N, (a + 1) * N)
             proj = banks.tile([P, N], F32, name=f"proj{a}")
             nc.tensor.matmul(
                 proj[:], weights[:, a * P : (a + 1) * P], nodes[:].indirect(offsets[:]), start=True, stop=True
             )
-            nc.vector.tensor_tensor(weighted[:, cols], proj[:], kw[:, cols], ALU.mult)
+            weighted_a = weighted[:, a * N : (a + 1) * N]
+            nc.vector.tensor_tensor(weighted_a, proj[:], u[:, a * N : (a + 1) * N], ALU.mult)
+            nc.vector.tensor_reduce(
+                summed[:, a * NODES : (a + 1) * NODES], weighted_a.rearrange("p (n k) -> p n k", k=K), AXIS.X, ALU.add
+            )
 
+        inverse_all = banks.tile([P, A * NODES], F32, name="inverse_all")
+        nc.tensor.matmul(inverse_all[:], ones[:], spread[:], start=True, stop=True)
+
+        nc.vector.tensor_tensor(summed[:], summed[:], inverse_all[:], ALU.mult)
         result = held.tile([P, NODES], F32, name="result")
-        nc.vector.tensor_reduce(
-            result[:], weighted[:].rearrange("p (a n k) -> p n a k", a=A, k=K), AXIS.XY, ALU.add
-        )
+        nc.vector.tensor_reduce(result[:], summed[:].rearrange("p (a n) -> p n a", a=A), AXIS.X, ALU.add)
         nc.sync.dma_start(out, result[:])

@@ -17,6 +17,7 @@ A = 4
 DIST = (0.0, 1.0)
 SIGN = (-1.0, 1.0)
 SHIFT = tuple(SIGN[a % 2] - 2.0 * DIST[a // 2] ** 2 for a in range(A))
+WARM_UP = 8
 
 FLOPS = 2 * P * (A * P) * N
 
@@ -89,6 +90,10 @@ def tile_nolayer_kernel(tc, table, w, d_dists, d_phi, offs, out):
             inverse[:].unsqueeze(2).to_broadcast([NODES, A, NODES]),
             ALU.mult,
         )
+
+        unread = banks.tile([P, A * P], F32, name="unread")
+        for repeat in range(WARM_UP):
+            nc.tensor.matmul(unread[:], weights[:, :P], weights[:], start=True, stop=True)
 
         weighted = held.tile([P, A * N], F32, name="weighted")
         summed = held.tile([P, A * NODES], F32, name="summed")

@@ -17,7 +17,6 @@ A = 4
 DIST = (0.0, 1.0)
 SIGN = (-1.0, 1.0)
 SHIFT = tuple(SIGN[a % 2] - 2.0 * DIST[a // 2] ** 2 for a in range(A))
-WARM_UP = 8
 
 FLOPS = 2 * P * (A * P) * N
 
@@ -45,6 +44,20 @@ def exponentials(nc, x):
         x_a = x[:, a * cols : (a + 1) * cols]
         nc.scalar.activation(x_a, x_a, FUNC.Exp, scale=-2.0, bias=SHIFT[a])
     return x
+
+
+def add_neighbours(nc, pool, engine, sums, products, label):
+    by_node = products.rearrange("p (n k) -> p n k", k=K)
+    if engine is nc.vector:
+        engine.tensor_reduce(sums, by_node, AXIS.X, ALU.add)
+        return
+    width = K // 2
+    while width > 1:
+        halved = pool.tile([P, NODES * width], F32, name=f"{label}_{width}")[:].rearrange("p (n k) -> p n k", k=width)
+        engine.tensor_tensor(halved, by_node[:, :, :width], by_node[:, :, width:], ALU.add)
+        by_node = halved
+        width //= 2
+    engine.tensor_tensor(sums.unsqueeze(2), by_node[:, :, :1], by_node[:, :, 1:], ALU.add)
 
 
 def tile_nolayer_kernel(tc, table, w, d_dists, d_phi, offs, out):
@@ -91,10 +104,6 @@ def tile_nolayer_kernel(tc, table, w, d_dists, d_phi, offs, out):
             ALU.mult,
         )
 
-        unread = banks.tile([P, A * P], F32, name="unread")
-        for repeat in range(WARM_UP):
-            nc.tensor.matmul(unread[:], weights[:, :P], weights[:], start=True, stop=True)
-
         weighted = held.tile([P, A * N], F32, name="weighted")
         summed = held.tile([P, A * NODES], F32, name="summed")
         for a in range(A):
@@ -104,9 +113,8 @@ def tile_nolayer_kernel(tc, table, w, d_dists, d_phi, offs, out):
             )
             weighted_a = weighted[:, a * N : (a + 1) * N]
             nc.vector.tensor_tensor(weighted_a, proj[:], u[:, a * N : (a + 1) * N], ALU.mult)
-            nc.vector.tensor_reduce(
-                summed[:, a * NODES : (a + 1) * NODES], weighted_a.rearrange("p (n k) -> p n k", k=K), AXIS.X, ALU.add
-            )
+            adder = nc.gpsimd if a < A // 2 else nc.vector
+            add_neighbours(nc, held, adder, summed[:, a * NODES : (a + 1) * NODES], weighted_a, f"halved{a}")
 
         inverse_all = banks.tile([P, A * NODES], F32, name="inverse_all")
         nc.tensor.matmul(inverse_all[:], ones[:], spread[:], start=True, stop=True)

@@ -113,7 +113,7 @@ def tile_nolayer_kernel(tc, table, w, d_dists, d_phi, offs, out):
             )
             weighted_a = weighted[:, a * N : (a + 1) * N]
             nc.vector.tensor_tensor(weighted_a, proj[:], u[:, a * N : (a + 1) * N], ALU.mult)
-            adder = nc.gpsimd if a < A // 2 else nc.vector
+            adder = nc.gpsimd if a == 0 else nc.vector
             add_neighbours(nc, held, adder, summed[:, a * NODES : (a + 1) * NODES], weighted_a, f"halved{a}")
 
         inverse_all = banks.tile([P, A * NODES], F32, name="inverse_all")

@@ -21,10 +21,8 @@ SHIFT = tuple(SIGN[a % 2] - 2.0 * DIST[a // 2] ** 2 for a in range(A))
 FLOPS = 2 * P * (A * P) * N
 
 
-def weight_exponents(nc, pool, phi, dist, engines, label):
-    rows, cols = phi.shape
-    half_sin = pool.tile([rows, cols], F32, name=label + "_half_sin")
-    nc.scalar.activation(half_sin[:], phi[:], FUNC.Sin, scale=0.5)
+def weight_exponents(nc, pool, half_sin, dist, engines, label):
+    rows, cols = half_sin.shape
     sin2 = pool.tile([rows, cols], F32, name=label + "_sin2")
     nc.vector.tensor_tensor(sin2[:], half_sin[:], half_sin[:], ALU.mult)
     gaps = [pool.tile([rows, cols], F32, name=f"{label}_gap{i}") for i in range(2)]
@@ -36,6 +34,13 @@ def weight_exponents(nc, pool, phi, dist, engines, label):
         add_or_subtract = ALU.add if SIGN[q] > 0 else ALU.subtract
         engines[i].tensor_tensor(x[:, a * cols : (a + 1) * cols], gaps[i][:], sin2[:], add_or_subtract)
     return x
+
+
+def to_all_partitions(nc, banks, packed, identity, label):
+    bank = banks.tile([P, N], F32, name=label)
+    for c in range(N // P):
+        nc.tensor.transpose(bank[:, c * P : (c + 1) * P], packed[:, c : c + 1].to_broadcast([P, P]), identity[:])
+    return bank[:].rearrange("m (c p) -> m p c", p=P)
 
 
 def exponentials(nc, x):
@@ -66,10 +71,10 @@ def tile_nolayer_kernel(tc, table, w, d_dists, d_phi, offs, out):
         tc.tile_pool(name="held", bufs=1) as held,
         tc.psum_pool(name="banks", bufs=1) as banks,
     ):
-        phi = held.tile([P, N], F32, name="phi")
-        nc.sync.dma_start(phi[:], d_phi.broadcast_to([P, N]))
-        dist = held.tile([P, N], F32, name="dist")
-        nc.scalar.dma_start(dist[:], d_dists.broadcast_to([P, N]))
+        phi_packed = held.tile([P, N // P], F32, name="phi_packed")
+        nc.sync.dma_start(phi_packed[:], d_phi.rearrange("o (p c) -> (o p) c", p=P))
+        dist_packed = held.tile([P, N // P], F32, name="dist_packed")
+        nc.scalar.dma_start(dist_packed[:], d_dists.rearrange("o (p c) -> (o p) c", p=P))
         phi_by_node = held.tile([NODES, K], F32, name="phi_by_node")
         nc.sync.dma_start(phi_by_node[:], d_phi.rearrange("o (n k) -> (o n) k", k=K))
         dist_by_node = held.tile([NODES, K], F32, name="dist_by_node")
@@ -88,8 +93,17 @@ def tile_nolayer_kernel(tc, table, w, d_dists, d_phi, offs, out):
         spread = held.tile([P, A * NODES], F32, name="spread")
         nc.gpsimd.memset(spread[:], 0.0)
 
-        x_by_node = weight_exponents(nc, held, phi_by_node, dist_by_node, (nc.vector, nc.vector), "node")
-        x = weight_exponents(nc, held, phi, dist, (nc.vector, nc.gpsimd), "all")
+        phi_all = to_all_partitions(nc, banks, phi_packed, identity, "phi_all")
+        dist_all = to_all_partitions(nc, banks, dist_packed, identity, "dist_all")
+        half_sin_by_node = held.tile([NODES, K], F32, name="half_sin_by_node")
+        nc.scalar.activation(half_sin_by_node[:], phi_by_node[:], FUNC.Sin, scale=0.5)
+        half_sin = held.tile([P, N], F32, name="half_sin")
+        nc.scalar.activation(half_sin[:].rearrange("m (p c) -> m p c", p=P), phi_all, FUNC.Sin, scale=0.5)
+        dist = held.tile([P, N], F32, name="dist")
+        nc.vector.tensor_copy(dist[:].rearrange("m (p c) -> m p c", p=P), dist_all)
+
+        x_by_node = weight_exponents(nc, held, half_sin_by_node, dist_by_node, (nc.vector, nc.vector), "node")
+        x = weight_exponents(nc, held, half_sin, dist, (nc.vector, nc.gpsimd), "all")
         u_by_node = exponentials(nc, x_by_node)
         u = exponentials(nc, x)
 

@@ -1,5 +1,5 @@
 import concourse.mybir as mybir
-from concourse.masks import make_identity
+from concourse.masks import make_block_diagonal, make_identity
 
 F32 = mybir.dt.float32
 BF16 = mybir.dt.bfloat16
@@ -14,41 +14,12 @@ N = 512
 NODES = 64
 K = 8
 A = 4
+C = N // P
+H = K // C
 DIST = (0.0, 1.0)
 SIGN = (-1.0, 1.0)
-SHIFT = tuple(SIGN[a % 2] - 2.0 * DIST[a // 2] ** 2 for a in range(A))
 
 FLOPS = 2 * P * (A * P) * N
-
-
-def weight_exponents(nc, pool, half_sin, dist, engines, label):
-    rows, cols = half_sin.shape
-    sin2 = pool.tile([rows, cols], F32, name=label + "_sin2")
-    nc.vector.tensor_tensor(sin2[:], half_sin[:], half_sin[:], ALU.mult)
-    gaps = [pool.tile([rows, cols], F32, name=f"{label}_gap{i}") for i in range(2)]
-    for i in range(2):
-        nc.vector.scalar_tensor_tensor(gaps[i][:], dist[:], -2.0 * DIST[i], dist[:], ALU.add, ALU.mult)
-    x = pool.tile([rows, A * cols], F32, name=label + "_x")
-    for a in range(A):
-        i, q = divmod(a, 2)
-        add_or_subtract = ALU.add if SIGN[q] > 0 else ALU.subtract
-        engines[i].tensor_tensor(x[:, a * cols : (a + 1) * cols], gaps[i][:], sin2[:], add_or_subtract)
-    return x
-
-
-def to_all_partitions(nc, banks, packed, identity, label):
-    bank = banks.tile([P, N], F32, name=label)
-    for c in range(N // P):
-        nc.tensor.transpose(bank[:, c * P : (c + 1) * P], packed[:, c : c + 1].to_broadcast([P, P]), identity[:])
-    return bank[:].rearrange("m (c p) -> m p c", p=P)
-
-
-def exponentials(nc, x):
-    cols = x.shape[1] // A
-    for a in range(A):
-        x_a = x[:, a * cols : (a + 1) * cols]
-        nc.scalar.activation(x_a, x_a, FUNC.Exp, scale=-2.0, bias=SHIFT[a])
-    return x
 
 
 def add_neighbours(nc, pool, engine, sums, products, label):
@@ -69,16 +40,13 @@ def tile_nolayer_kernel(tc, table, w, d_dists, d_phi, offs, out):
     nc = tc.nc
     with (
         tc.tile_pool(name="held", bufs=1) as held,
-        tc.psum_pool(name="banks", bufs=1) as banks,
+        tc.psum_pool(name="banks", bufs=A) as banks,
+        tc.psum_pool(name="lone", bufs=1) as lone,
     ):
-        phi_packed = held.tile([P, N // P], F32, name="phi_packed")
-        nc.sync.dma_start(phi_packed[:], d_phi.rearrange("o (p c) -> (o p) c", p=P))
-        dist_packed = held.tile([P, N // P], F32, name="dist_packed")
-        nc.scalar.dma_start(dist_packed[:], d_dists.rearrange("o (p c) -> (o p) c", p=P))
-        phi_by_node = held.tile([NODES, K], F32, name="phi_by_node")
-        nc.sync.dma_start(phi_by_node[:], d_phi.rearrange("o (n k) -> (o n) k", k=K))
-        dist_by_node = held.tile([NODES, K], F32, name="dist_by_node")
-        nc.scalar.dma_start(dist_by_node[:], d_dists.rearrange("o (n k) -> (o n) k", k=K))
+        phi = held.tile([P, C], F32, name="phi")
+        nc.sync.dma_start(phi[:], d_phi.rearrange("o (p c) -> (o p) c", c=C))
+        dist = held.tile([P, C], F32, name="dist")
+        nc.scalar.dma_start(dist[:], d_dists.rearrange("o (p c) -> (o p) c", c=C))
         offsets = held.tile([P, N // 16], U16, name="offsets")
         nc.sync.dma_start(offsets[:], offs)
         weights = held.tile([P, A * P], BF16, name="weights")
@@ -88,52 +56,78 @@ def tile_nolayer_kernel(tc, table, w, d_dists, d_phi, offs, out):
 
         identity = held.tile([P, P], F32, name="identity")
         make_identity(nc, identity[:])
-        ones = held.tile([P, P], F32, name="ones")
-        nc.gpsimd.memset(ones[:], 1.0)
-        spread = held.tile([P, A * NODES], F32, name="spread")
-        nc.gpsimd.memset(spread[:], 0.0)
+        same_node = held.tile([P, P], F32, name="same_node")
+        make_block_diagonal(nc, same_node[:], H)
 
-        phi_all = to_all_partitions(nc, banks, phi_packed, identity, "phi_all")
-        dist_all = to_all_partitions(nc, banks, dist_packed, identity, "dist_all")
-        half_sin_by_node = held.tile([NODES, K], F32, name="half_sin_by_node")
-        nc.scalar.activation(half_sin_by_node[:], phi_by_node[:], FUNC.Sin, scale=0.5)
-        half_sin = held.tile([P, N], F32, name="half_sin")
-        nc.scalar.activation(half_sin[:].rearrange("m (p c) -> m p c", p=P), phi_all, FUNC.Sin, scale=0.5)
-        dist = held.tile([P, N], F32, name="dist")
-        nc.vector.tensor_copy(dist[:].rearrange("m (p c) -> m p c", p=P), dist_all)
+        half_sin = held.tile([P, C], F32, name="half_sin")
+        nc.scalar.activation(half_sin[:], phi[:], FUNC.Sin, scale=0.5)
+        sin2 = held.tile([P, C], F32, name="sin2")
+        nc.vector.tensor_tensor(sin2[:], half_sin[:], half_sin[:], ALU.mult)
+        gaps = held.tile([P, 2 * C], F32, name="gaps")
+        for i in range(2):
+            nc.vector.scalar_tensor_tensor(
+                gaps[:, i * C : (i + 1) * C], dist[:], -2.0 * DIST[i], dist[:], ALU.add, ALU.mult
+            )
+        x = held.tile([P, A * C], F32, name="x")
+        for q in range(2):
+            nc.vector.tensor_tensor(
+                x[:].rearrange("p (i q c) -> p i q c", i=2, q=2)[:, :, q, :],
+                gaps[:].rearrange("p (i c) -> p i c", i=2),
+                sin2[:].unsqueeze(1).to_broadcast([P, 2, C]),
+                ALU.add if SIGN[q] > 0 else ALU.subtract,
+            )
 
-        x_by_node = weight_exponents(nc, held, half_sin_by_node, dist_by_node, (nc.vector, nc.vector), "node")
-        x = weight_exponents(nc, held, half_sin, dist, (nc.vector, nc.gpsimd), "all")
-        u_by_node = exponentials(nc, x_by_node)
-        u = exponentials(nc, x)
+        x_all = []
+        for a in range(A):
+            x_all.append(banks.tile([P, N], F32, name=f"x_all{a}", tag="bank"))
+            for c in range(C):
+                column = a * C + c
+                nc.tensor.transpose(
+                    x_all[a][:, c * P : (c + 1) * P], x[:, column : column + 1].to_broadcast([P, P]), identity[:]
+                )
 
-        total = held.tile([NODES, A], F32, name="total")
-        nc.vector.tensor_reduce(total[:], u_by_node[:].rearrange("n (a k) -> n a k", k=K), AXIS.X, ALU.add)
-        inverse = held.tile([NODES, A], F32, name="inverse")
+        u_small = held.tile([P, A * C], F32, name="u_small")
+        nc.scalar.activation(u_small[:], x[:], FUNC.Exp, scale=-2.0)
+        partial = held.tile([P, A], F32, name="partial")
+        nc.vector.tensor_reduce(partial[:], u_small[:].rearrange("p (a c) -> p a c", a=A), AXIS.X, ALU.add)
+        total = lone.tile([P, A], F32, name="total")
+        nc.tensor.matmul(total[:], same_node[:], partial[:], start=True, stop=True)
+        inverse = held.tile([P, A], F32, name="inverse")
         nc.vector.reciprocal(inverse[:], total[:])
-        nc.vector.tensor_tensor(
-            spread[:NODES].rearrange("n (a c) -> n a c", a=A),
-            identity[:NODES, :NODES].unsqueeze(1).to_broadcast([NODES, A, NODES]),
-            inverse[:].unsqueeze(2).to_broadcast([NODES, A, NODES]),
-            ALU.mult,
-        )
+
+        u = held.tile([P, A * N], F32, name="u")
+        for a in range(A):
+            nc.scalar.activation(u[:, a * N : (a + 1) * N], x_all[a][:], FUNC.Exp, scale=-2.0)
 
         weighted = held.tile([P, A * N], F32, name="weighted")
         summed = held.tile([P, A * NODES], F32, name="summed")
         for a in range(A):
-            proj = banks.tile([P, N], F32, name=f"proj{a}")
+            proj = banks.tile([P, N], F32, name="proj", tag="bank")
             nc.tensor.matmul(
                 proj[:], weights[:, a * P : (a + 1) * P], nodes[:].indirect(offsets[:]), start=True, stop=True
             )
             weighted_a = weighted[:, a * N : (a + 1) * N]
-            nc.vector.tensor_tensor(weighted_a, proj[:], u[:, a * N : (a + 1) * N], ALU.mult)
+            nc.vector.tensor_tensor(
+                weighted_a.rearrange("m (p c) -> m p c", c=C),
+                proj[:].rearrange("m (p c) -> m p c", c=C),
+                u[:, a * N : (a + 1) * N].rearrange("m (c p) -> m p c", c=C),
+                ALU.mult,
+            )
             adder = nc.gpsimd if a == 0 else nc.vector
             add_neighbours(nc, held, adder, summed[:, a * NODES : (a + 1) * NODES], weighted_a, f"halved{a}")
 
-        inverse_all = banks.tile([P, A * NODES], F32, name="inverse_all")
-        nc.tensor.matmul(inverse_all[:], ones[:], spread[:], start=True, stop=True)
+        inverse_all = lone.tile([P, A * P], F32, name="inverse_all")
+        for a in range(A):
+            nc.tensor.transpose(
+                inverse_all[:, a * P : (a + 1) * P], inverse[:, a : a + 1].to_broadcast([P, P]), identity[:]
+            )
 
-        nc.vector.tensor_tensor(summed[:], summed[:], inverse_all[:], ALU.mult)
+        nc.vector.tensor_tensor(
+            summed[:].rearrange("m (a n) -> m a n", a=A),
+            summed[:].rearrange("m (a n) -> m a n", a=A),
+            inverse_all[:].rearrange("m (a n h) -> m a n h", a=A, h=H)[:, :, :, 0],
+            ALU.mult,
+        )
         result = held.tile([P, NODES], F32, name="result")
         nc.vector.tensor_reduce(result[:], summed[:].rearrange("p (a n) -> p n a", a=A), AXIS.X, ALU.add)
         nc.sync.dma_start(out, result[:])

@@ -101,20 +101,25 @@ def tile_nolayer_kernel(tc, table, w, d_dists, d_phi, offs, out):
 
         weighted = held.tile([P, A * N], F32, name="weighted")
         summed = held.tile([P, A * NODES], F32, name="summed")
-        for a in range(A):
-            proj = banks.tile([P, N], F32, name="proj", tag="bank")
-            nc.tensor.matmul(
-                proj[:], weights[:, a * P : (a + 1) * P], nodes[:].indirect(offsets[:]), start=True, stop=True
-            )
-            weighted_a = weighted[:, a * N : (a + 1) * N]
-            nc.vector.tensor_tensor(
-                weighted_a.rearrange("m (p c) -> m p c", c=C),
-                proj[:].rearrange("m (p c) -> m p c", c=C),
-                u[:, a * N : (a + 1) * N].rearrange("m (c p) -> m p c", c=C),
-                ALU.mult,
-            )
-            adder = nc.gpsimd if a == 0 else nc.vector
-            add_neighbours(nc, held, adder, summed[:, a * NODES : (a + 1) * NODES], weighted_a, f"halved{a}")
+        for step in range(A + 1):
+            if step < A:
+                a = step
+                proj = banks.tile([P, N], F32, name="proj", tag="bank")
+                nc.tensor.matmul(
+                    proj[:], weights[:, a * P : (a + 1) * P], nodes[:].indirect(offsets[:]), start=True, stop=True
+                )
+                nc.vector.tensor_tensor(
+                    weighted[:, a * N : (a + 1) * N].rearrange("m (p c) -> m p c", c=C),
+                    proj[:].rearrange("m (p c) -> m p c", c=C),
+                    u[:, a * N : (a + 1) * N].rearrange("m (c p) -> m p c", c=C),
+                    ALU.mult,
+                )
+            if step > 0:
+                a = step - 1
+                adder = nc.gpsimd if a == 0 else nc.vector
+                add_neighbours(
+                    nc, held, adder, summed[:, a * NODES : (a + 1) * NODES], weighted[:, a * N : (a + 1) * N], f"halved{a}"
+                )
 
         inverse_all = lone.tile([P, A * P], F32, name="inverse_all")
         for a in range(A):

@@ -127,12 +127,13 @@ def tile_nolayer_kernel(tc, table, w, d_dists, d_phi, offs, out):
                 inverse_all[:, a * P : (a + 1) * P], inverse[:, a : a + 1].to_broadcast([P, P]), identity[:]
             )
 
-        nc.vector.tensor_tensor(
-            summed[:].rearrange("m (a n) -> m a n", a=A),
-            summed[:].rearrange("m (a n) -> m a n", a=A),
-            inverse_all[:].rearrange("m (a n h) -> m a n h", a=A, h=H)[:, :, :, 0],
-            ALU.mult,
-        )
+        for first, last in ((0, A - 1), (A - 1, A)):
+            nc.vector.tensor_tensor(
+                summed[:].rearrange("m (a n) -> m a n", a=A)[:, first:last],
+                summed[:].rearrange("m (a n) -> m a n", a=A)[:, first:last],
+                inverse_all[:].rearrange("m (a n h) -> m a n h", a=A, h=H)[:, first:last, :, 0],
+                ALU.mult,
+            )
         result = held.tile([P, NODES], F32, name="result")
         nc.vector.tensor_reduce(result[:], summed[:].rearrange("p (a n) -> p n a", a=A), AXIS.X, ALU.add)
         nc.sync.dma_start(out, result[:])

@@ -36,6 +36,14 @@ def add_neighbours(nc, pool, engine, sums, products, label):
     engine.tensor_tensor(sums.unsqueeze(2), by_node[:, :, :1], by_node[:, :, 1:], ALU.add)
 
 
+def to_all_partitions(nc, pool, small, identity, label):
+    columns = small.shape[1]
+    copies = pool.tile([P, columns * P], F32, name=label, tag="bank")
+    for c in range(columns):
+        nc.tensor.transpose(copies[:, c * P : (c + 1) * P], small[:, c : c + 1].to_broadcast([P, P]), identity[:])
+    return copies
+
+
 def tile_nolayer_kernel(tc, table, w, d_dists, d_phi, offs, out):
     nc = tc.nc
     with (
@@ -77,14 +85,8 @@ def tile_nolayer_kernel(tc, table, w, d_dists, d_phi, offs, out):
                 ALU.add if SIGN[q] > 0 else ALU.subtract,
             )
 
-        x_all = []
-        for a in range(A):
-            x_all.append(banks.tile([P, N], F32, name=f"x_all{a}", tag="bank"))
-            for c in range(C):
-                column = a * C + c
-                nc.tensor.transpose(
-                    x_all[a][:, c * P : (c + 1) * P], x[:, column : column + 1].to_broadcast([P, P]), identity[:]
-                )
+        dist_all = to_all_partitions(nc, banks, dist[:], identity, "dist_all")
+        x_all = [to_all_partitions(nc, banks, x[:, a * C : (a + 1) * C], identity, f"x_all{a}") for a in range(2)]
 
         u_small = held.tile([P, A * C], F32, name="u_small")
         nc.scalar.activation(u_small[:], x[:], FUNC.Exp, scale=-2.0)
@@ -95,9 +97,12 @@ def tile_nolayer_kernel(tc, table, w, d_dists, d_phi, offs, out):
         inverse = held.tile([P, A], F32, name="inverse")
         nc.vector.reciprocal(inverse[:], total[:])
 
+        step_up = held.tile([P, N], F32, name="step_up")
+        nc.scalar.activation(step_up[:], dist_all[:], FUNC.Exp, scale=4.0 * (DIST[1] - DIST[0]))
         u = held.tile([P, A * N], F32, name="u")
-        for a in range(A):
+        for a, engine in ((0, nc.vector), (1, nc.gpsimd)):
             nc.scalar.activation(u[:, a * N : (a + 1) * N], x_all[a][:], FUNC.Exp, scale=-2.0)
+            engine.tensor_tensor(u[:, (a + 2) * N : (a + 3) * N], u[:, a * N : (a + 1) * N], step_up[:], ALU.mult)
 
         weighted = held.tile([P, A * N], F32, name="weighted")
         summed = held.tile([P, A * NODES], F32, name="summed")

@@ -22,20 +22,6 @@ SIGN = (-1.0, 1.0)
 FLOPS = 2 * P * (A * P) * N
 
 
-def add_neighbours(nc, pool, engine, sums, products, label):
-    by_node = products.rearrange("p (n k) -> p n k", k=K)
-    if engine is nc.vector:
-        engine.tensor_reduce(sums, by_node, AXIS.X, ALU.add)
-        return
-    width = K // 2
-    while width > 1:
-        halved = pool.tile([P, NODES * width], F32, name=f"{label}_{width}")[:].rearrange("p (n k) -> p n k", k=width)
-        engine.tensor_tensor(halved, by_node[:, :, :width], by_node[:, :, width:], ALU.add)
-        by_node = halved
-        width //= 2
-    engine.tensor_tensor(sums.unsqueeze(2), by_node[:, :, :1], by_node[:, :, 1:], ALU.add)
-
-
 def to_all_partitions(nc, pool, small, identity, label):
     columns = small.shape[1]
     copies = pool.tile([P, columns * P], F32, name=label, tag="bank")
@@ -48,7 +34,7 @@ def tile_nolayer_kernel(tc, table, w, d_dists, d_phi, offs, out):
     nc = tc.nc
     with (
         tc.tile_pool(name="held", bufs=1) as held,
-        tc.psum_pool(name="banks", bufs=A) as banks,
+        tc.psum_pool(name="banks", bufs=A + 1) as banks,
         tc.psum_pool(name="lone", bufs=1) as lone,
     ):
         phi = held.tile([P, C], F32, name="phi")
@@ -92,10 +78,6 @@ def tile_nolayer_kernel(tc, table, w, d_dists, d_phi, offs, out):
         nc.scalar.activation(u_small[:], x[:], FUNC.Exp, scale=-2.0)
         partial = held.tile([P, A], F32, name="partial")
         nc.vector.tensor_reduce(partial[:], u_small[:].rearrange("p (a c) -> p a c", a=A), AXIS.X, ALU.add)
-        total = lone.tile([P, A], F32, name="total")
-        nc.tensor.matmul(total[:], same_node[:], partial[:], start=True, stop=True)
-        inverse = held.tile([P, A], F32, name="inverse")
-        nc.vector.reciprocal(inverse[:], total[:])
 
         step_up = held.tile([P, N], F32, name="step_up")
         nc.scalar.activation(step_up[:], dist_all[:], FUNC.Exp, scale=4.0 * (DIST[1] - DIST[0]))
@@ -105,40 +87,69 @@ def tile_nolayer_kernel(tc, table, w, d_dists, d_phi, offs, out):
             engine.tensor_tensor(u[:, (a + 2) * N : (a + 3) * N], u[:, a * N : (a + 1) * N], step_up[:], ALU.mult)
 
         weighted = held.tile([P, A * N], F32, name="weighted")
-        summed = held.tile([P, A * NODES], F32, name="summed")
-        for step in range(A + 1):
-            if step < A:
-                a = step
-                proj = banks.tile([P, N], F32, name="proj", tag="bank")
-                nc.tensor.matmul(
-                    proj[:], weights[:, a * P : (a + 1) * P], nodes[:].indirect(offsets[:]), start=True, stop=True
-                )
-                nc.vector.tensor_tensor(
-                    weighted[:, a * N : (a + 1) * N].rearrange("m (p c) -> m p c", c=C),
-                    proj[:].rearrange("m (p c) -> m p c", c=C),
-                    u[:, a * N : (a + 1) * N].rearrange("m (c p) -> m p c", c=C),
-                    ALU.mult,
-                )
-            if step > 0:
-                a = step - 1
-                adder = nc.gpsimd if a == 0 else nc.vector
-                add_neighbours(
-                    nc, held, adder, summed[:, a * NODES : (a + 1) * NODES], weighted[:, a * N : (a + 1) * N], f"halved{a}"
-                )
-
-        inverse_all = lone.tile([P, A * P], F32, name="inverse_all")
         for a in range(A):
-            nc.tensor.transpose(
-                inverse_all[:, a * P : (a + 1) * P], inverse[:, a : a + 1].to_broadcast([P, P]), identity[:]
+            proj = banks.tile([P, N], F32, name="proj", tag="bank")
+            nc.tensor.matmul(
+                proj[:], weights[:, a * P : (a + 1) * P], nodes[:].indirect(offsets[:]), start=True, stop=True
             )
-
-        for first, last in ((0, A - 1), (A - 1, A)):
+            if a == A - 1:
+                total = lone.tile([P, A], F32, name="total")
+                nc.tensor.matmul(total[:], same_node[:], partial[:], start=True, stop=True)
+                inverse = held.tile([P, A], F32, name="inverse")
+                nc.vector.reciprocal(inverse[:], total[:])
             nc.vector.tensor_tensor(
-                summed[:].rearrange("m (a n) -> m a n", a=A)[:, first:last],
-                summed[:].rearrange("m (a n) -> m a n", a=A)[:, first:last],
-                inverse_all[:].rearrange("m (a n h) -> m a n h", a=A, h=H)[:, first:last, :, 0],
+                weighted[:, a * N : (a + 1) * N].rearrange("m (p c) -> m p c", c=C),
+                proj[:].rearrange("m (p c) -> m p c", c=C),
+                u[:, a * N : (a + 1) * N].rearrange("m (c p) -> m p c", c=C),
                 ALU.mult,
             )
+
+        on_tensor, on_vector = range(2), range(2, A)
+        outer = lone.tile([P, NODES], F32, name="outer")
+        for a in on_tensor:
+            halves = banks.tile([P, P], F32, name="halves", tag="bank")
+            for c in range(C):
+                nc.tensor.matmul(
+                    halves[:],
+                    weighted[:, a * N : (a + 1) * N].rearrange("m (p c) -> m p c", c=C)[:, :, c],
+                    identity[:],
+                    is_transpose=True,
+                    start=c == 0,
+                    stop=c == C - 1,
+                )
+            divided = held.tile([P, P], F32, name=f"divided{a}")
+            nc.scalar.activation(divided[:], halves[:], FUNC.Copy, scale=inverse[:, a : a + 1])
+            nc.tensor.matmul(
+                outer[:],
+                divided[:],
+                same_node[:].rearrange("p (n h) -> p n h", h=H)[:, :, 0],
+                start=a == on_tensor[0],
+                stop=a == on_tensor[-1],
+            )
+
+        inverse_all = lone.tile([P, len(on_vector) * P], F32, name="inverse_all")
+        summed = held.tile([P, len(on_vector) * NODES], F32, name="summed")
+        quotients = held.tile([P, len(on_vector) * NODES], F32, name="quotients")
+        for i, a in enumerate(on_vector):
+            nc.tensor.transpose(
+                inverse_all[:, i * P : (i + 1) * P], inverse[:, a : a + 1].to_broadcast([P, P]), identity[:]
+            )
+        for i, a in enumerate(on_vector):
+            nc.vector.tensor_reduce(
+                summed[:, i * NODES : (i + 1) * NODES],
+                weighted[:, a * N : (a + 1) * N].rearrange("p (n k) -> p n k", k=K),
+                AXIS.X,
+                ALU.add,
+            )
+        for i, a in enumerate(on_vector):
+            nc.vector.tensor_tensor(
+                quotients[:, i * NODES : (i + 1) * NODES],
+                summed[:, i * NODES : (i + 1) * NODES],
+                inverse_all[:, i * P : (i + 1) * P].rearrange("m (n h) -> m n h", h=H)[:, :, 0],
+                ALU.mult,
+            )
+        first_three = held.tile([P, NODES], F32, name="first_three")
+        nc.vector.tensor_tensor(first_three[:], quotients[:, :NODES], outer[:], ALU.add)
         result = held.tile([P, NODES], F32, name="result")
-        nc.vector.tensor_reduce(result[:], summed[:].rearrange("p (a n) -> p n a", a=A), AXIS.X, ALU.add)
+        nc.vector.tensor_tensor(result[:], first_three[:], quotients[:, NODES:], ALU.add)
         nc.sync.dma_start(out, result[:])

import concourse.mybir as mybir
from concourse.masks import make_block_diagonal, make_identity

F32 = mybir.dt.float32
BF16 = mybir.dt.bfloat16
U16 = mybir.dt.uint16
FUNC = mybir.ActivationFunctionType
ALU = mybir.AluOpType
AXIS = mybir.AxisListType

P = 128
S = 4096
N = 512
NODES = 64
K = 8
A = 4
C = N // P
H = K // C
DIST = (0.0, 1.0)
SIGN = (-1.0, 1.0)

FLOPS = 2 * P * (A * P) * N


def to_all_partitions(nc, pool, small, identity, label):
    columns = small.shape[1]
    copies = pool.tile([P, columns * P], F32, name=label, tag="bank")
    for c in range(columns):
        nc.tensor.transpose(copies[:, c * P : (c + 1) * P], small[:, c : c + 1].to_broadcast([P, P]), identity[:])
    return copies


def tile_nolayer_kernel(tc, table, w, d_dists, d_phi, offs, out):
    nc = tc.nc
    with (
        tc.tile_pool(name="held", bufs=1) as held,
        tc.psum_pool(name="banks", bufs=A + 1) as banks,
        tc.psum_pool(name="lone", bufs=1) as lone,
    ):
        phi = held.tile([P, C], F32, name="phi")
        nc.sync.dma_start(phi[:], d_phi.rearrange("o (p c) -> (o p) c", c=C))
        dist = held.tile([P, C], F32, name="dist")
        nc.scalar.dma_start(dist[:], d_dists.rearrange("o (p c) -> (o p) c", c=C))
        offsets = held.tile([P, N // 16], U16, name="offsets")
        nc.sync.dma_start(offsets[:], offs)
        weights = held.tile([P, A * P], BF16, name="weights")
        nc.scalar.dma_start(weights[:], w)
        nodes = held.tile([P, S], BF16, name="nodes")
        nc.sync.dma_start(nodes[:], table)

        identity = held.tile([P, P], F32, name="identity")
        make_identity(nc, identity[:])
        same_node = held.tile([P, P], F32, name="same_node")
        make_block_diagonal(nc, same_node[:], H)

        half_sin = held.tile([P, C], F32, name="half_sin")
        nc.scalar.activation(half_sin[:], phi[:], FUNC.Sin, scale=0.5)
        sin2 = held.tile([P, C], F32, name="sin2")
        nc.vector.tensor_tensor(sin2[:], half_sin[:], half_sin[:], ALU.mult)
        gaps = held.tile([P, 2 * C], F32, name="gaps")
        for i in range(2):
            nc.vector.scalar_tensor_tensor(
                gaps[:, i * C : (i + 1) * C], dist[:], -2.0 * DIST[i], dist[:], ALU.add, ALU.mult
            )
        x = held.tile([P, A * C], F32, name="x")
        for q in range(2):
            nc.vector.tensor_tensor(
                x[:].rearrange("p (i q c) -> p i q c", i=2, q=2)[:, :, q, :],
                gaps[:].rearrange("p (i c) -> p i c", i=2),
                sin2[:].unsqueeze(1).to_broadcast([P, 2, C]),
                ALU.add if SIGN[q] > 0 else ALU.subtract,
            )

        dist_all = to_all_partitions(nc, banks, dist[:], identity, "dist_all")
        x_all = [to_all_partitions(nc, banks, x[:, a * C : (a + 1) * C], identity, f"x_all{a}") for a in range(2)]

        u_small = held.tile([P, A * C], F32, name="u_small")
        nc.scalar.activation(u_small[:], x[:], FUNC.Exp, scale=-2.0)
        partial = held.tile([P, A], F32, name="partial")
        nc.vector.tensor_reduce(partial[:], u_small[:].rearrange("p (a c) -> p a c", a=A), AXIS.X, ALU.add)

        step_up = held.tile([P, N], F32, name="step_up")
        nc.scalar.activation(step_up[:], dist_all[:], FUNC.Exp, scale=4.0 * (DIST[1] - DIST[0]))
        u = held.tile([P, A * N], F32, name="u")
        for a, engine in ((0, nc.vector), (1, nc.gpsimd)):
            nc.scalar.activation(u[:, a * N : (a + 1) * N], x_all[a][:], FUNC.Exp, scale=-2.0)
            engine.tensor_tensor(u[:, (a + 2) * N : (a + 3) * N], u[:, a * N : (a + 1) * N], step_up[:], ALU.mult)

        weighted = held.tile([P, A * N], F32, name="weighted")
        for a in range(A):
            proj = banks.tile([P, N], F32, name="proj", tag="bank")
            nc.tensor.matmul(
                proj[:], weights[:, a * P : (a + 1) * P], nodes[:].indirect(offsets[:]), start=True, stop=True
            )
            if a == A - 1:
                total = lone.tile([P, A], F32, name="total")
                nc.tensor.matmul(total[:], same_node[:], partial[:], start=True, stop=True)
                inverse = held.tile([P, A], F32, name="inverse")
                nc.vector.reciprocal(inverse[:], total[:])
            nc.vector.tensor_tensor(
                weighted[:, a * N : (a + 1) * N].rearrange("m (p c) -> m p c", c=C),
                proj[:].rearrange("m (p c) -> m p c", c=C),
                u[:, a * N : (a + 1) * N].rearrange("m (c p) -> m p c", c=C),
                ALU.mult,
            )

        on_tensor, on_vector = range(2), range(2, A)
        outer = lone.tile([P, NODES], F32, name="outer")
        for a in on_tensor:
            halves = banks.tile([P, P], F32, name="halves", tag="bank")
            for c in range(C):
                nc.tensor.matmul(
                    halves[:],
                    weighted[:, a * N : (a + 1) * N].rearrange("m (p c) -> m p c", c=C)[:, :, c],
                    identity[:],
                    is_transpose=True,
                    start=c == 0,
                    stop=c == C - 1,
                )
            divided = held.tile([P, P], F32, name=f"divided{a}")
            nc.scalar.activation(divided[:], halves[:], FUNC.Copy, scale=inverse[:, a : a + 1])
            nc.tensor.matmul(
                outer[:],
                divided[:],
                same_node[:].rearrange("p (n h) -> p n h", h=H)[:, :, 0],
                start=a == on_tensor[0],
                stop=a == on_tensor[-1],
            )

        inverse_all = lone.tile([P, len(on_vector) * P], F32, name="inverse_all")
        summed = held.tile([P, len(on_vector) * NODES], F32, name="summed")
        quotients = held.tile([P, len(on_vector) * NODES], F32, name="quotients")
        for i, a in enumerate(on_vector):
            nc.tensor.transpose(
                inverse_all[:, i * P : (i + 1) * P], inverse[:, a : a + 1].to_broadcast([P, P]), identity[:]
            )
        for i, a in enumerate(on_vector):
            nc.vector.tensor_reduce(
                summed[:, i * NODES : (i + 1) * NODES],
                weighted[:, a * N : (a + 1) * N].rearrange("p (n k) -> p n k", k=K),
                AXIS.X,
                ALU.add,
            )
        for i, a in enumerate(on_vector):
            nc.vector.tensor_tensor(
                quotients[:, i * NODES : (i + 1) * NODES],
                summed[:, i * NODES : (i + 1) * NODES],
                inverse_all[:, i * P : (i + 1) * P].rearrange("m (n h) -> m n h", h=H)[:, :, 0],
                ALU.mult,
            )
        first_three = held.tile([P, NODES], F32, name="first_three")
        nc.vector.tensor_tensor(first_three[:], quotients[:, :NODES], outer[:], ALU.add)
        result = held.tile([P, NODES], F32, name="result")
        nc.vector.tensor_tensor(result[:], first_three[:], quotients[:, NODES:], ALU.add)
        nc.sync.dma_start(out, result[:])
